import numpy as np
import ml_dtypes


def mxq(x, axis, fmt="e4m3"):
    dtype, down = {"e4m3": (ml_dtypes.float8_e4m3fn, 7), "e5m2": (ml_dtypes.float8_e5m2, 14)}[fmt]
    v = np.moveaxis(np.asarray(x, np.float32).astype(ml_dtypes.bfloat16).astype(np.float64), axis, -1)
    blocks = v.reshape(v.shape[:-1] + (-1, 32))
    amax = np.abs(blocks).max(-1, keepdims=True)
    byte = np.maximum(np.where(amax > 0, np.frexp(amax)[1] - 1 + 127, 0) - down, 1)
    scale = np.exp2(byte - 127.0)
    codes = (blocks / scale).astype(np.float32).astype(dtype).astype(np.float64)
    return np.moveaxis((codes * scale).reshape(v.shape), -1, axis)


WIDE = False


def mx_kscale(k):
    if not WIDE:
        return np.ones(k)
    levels = np.array([10, -10, 5, -5, 0])
    if k % 512:
        return np.exp2(np.random.permutation(np.resize(levels, k // 32))).repeat(32)
    a = np.empty((k // 512, 16))
    for p in range(k // 512):
        a[p, :8] = np.random.permutation(np.resize(levels, 8))
        for g in range(8):
            far = levels[np.abs(levels - a[p, g]) >= 10]
            a[p, g + 8] = far[np.random.randint(len(far))]
    return np.exp2(a.ravel()).repeat(32)


BF16 = ml_dtypes.bfloat16


def bf(x):
    return np.asarray(x, np.float32).astype(BF16)


def f64(x):
    return np.asarray(x).astype(np.float64)


B, L, N, O = 2, 2, 1024, 512

LOOP = 1.0


def setup_inputs():
    s = mx_kscale(N)
    g = np.random.random((B, L, 1, N)) * 2.0
    mask = np.random.random((B, L, N, N)) * (4.0 / N) * g + np.eye(N) * np.random.random((B, L, N, 1)) * 2.0
    return {"x": bf(np.random.standard_normal((B, L, N, N)) * s),
            "mask": bf(mask),
            "weight": bf(np.random.standard_normal((N, O)) / np.sqrt(N) / s[:, None]),
            "bias": bf(np.random.standard_normal(O) * 0.3)}


def reference(x, mask, weight, bias):
    xf = f64(x).reshape(B * L, N, N)
    mf = f64(mask).reshape(B * L, N, N)
    eye = np.eye(N)
    m_sl = mf * (1.0 - eye) + LOOP * eye
    d = np.sum(m_sl, axis=1)
    inv_sqrt_d = 1.0 / np.sqrt(d)
    h = xf * inv_sqrt_d[:, :, None]
    out = np.maximum((mxq(h, 2, "e4m3") @ mxq(f64(weight), 0, "e4m3")) + f64(bias), 0.0)
    return out.reshape(B, L, N, O)

@@ -1,0 +1,389 @@
+from contextlib import ExitStack
+
+import concourse.mybir as mybir
+from concourse.masks import make_identity
+
+FP8X4 = mybir.dt.float8_e4m3fn_x4
+BF16 = mybir.dt.bfloat16
+F32 = mybir.dt.float32
+U32 = mybir.dt.uint32
+U8 = mybir.dt.uint8
+ALU = mybir.AluOpType
+ACT = mybir.ActivationFunctionType
+AX = mybir.AxisListType
+
+P = 128
+PACK = 4
+GRAPHS = 4
+NODES = 1024
+FEAT = 1024
+OUTF = 512
+PASSES = FEAT // (P * PACK)
+BLOCKS = FEAT // P
+SLICES = NODES // P
+PAIR = 2
+ROUNDS_PER_GRAPH = SLICES // PAIR
+ROUNDS = GRAPHS * ROUNDS_PER_GRAPH
+LEAD = 2
+CHUNKS = 4
+CHUNK_ROWS = 2
+SUM_COLS = 16
+SPREAD = P // SLICES
+CLOCK_REPEATS = 2
+RESIDENT = 3
+RESULT_BUFS = 12
+LOOP = 1.0
+FLOPS = 2 * GRAPHS * NODES * FEAT * OUTF
+
+
+def tile_gcn_t_kernel(tc, x, mask, weight, bias, out):
+    nc = tc.nc
+    x_view = x.rearrange("a b (p t) k -> (a b) p t k", t=SLICES)
+    out_view = out.rearrange("a b (p t) o -> (a b) p t o", t=SLICES)
+    mask_view = mask.rearrange("a b (c p t) i -> (a b) p c t i", c=CHUNKS, p=P, t=CHUNK_ROWS)
+    weight_view = weight.rearrange("(c p t) o -> p c t o", c=PASSES, t=PACK, p=P)
+    bias_view = bias.rearrange("(r n) -> r n", r=1)
+
+    with ExitStack() as ctx:
+        const = ctx.enter_context(tc.tile_pool(name="const", bufs=1))
+        mask_pool = ctx.enter_context(tc.tile_pool(name="mask_pool", bufs=RESIDENT))
+        x_pool = ctx.enter_context(tc.tile_pool(name="x_pool", bufs=RESIDENT))
+        work = ctx.enter_context(tc.tile_pool(name="work", bufs=LEAD + 1))
+        small = ctx.enter_context(tc.tile_pool(name="small", bufs=2))
+        result_pool = ctx.enter_context(tc.tile_pool(name="result_pool", bufs=RESULT_BUFS))
+        psum_t = ctx.enter_context(tc.psum_pool(name="psum_t", bufs=3))
+        psum_o = ctx.enter_context(tc.psum_pool(name="psum_o", bufs=4))
+        psum_d = ctx.enter_context(tc.psum_pool(name="psum_d", bufs=1))
+        ctx.enter_context(tc.manual_schedule())
+
+        mask_tiles = {}
+        x_tiles = {}
+        sum_banks = {}
+        spread_tiles = {}
+        root_tiles = {}
+        inv_sqrt_d = {}
+        scaled = {}
+        flipped = {}
+        grouped = {}
+        packed = {}
+        products = {}
+        results = {}
+
+        ident_f = const.tile([P, P], F32, name="ident_f")
+        make_identity(nc, ident_f[:])
+        one_col = const.tile([P, 1], F32, name="one_col")
+        nc.vector.memset(one_col[:], 1.0)
+        bias_row = const.tile([P, OUTF], BF16, name="bias_row")
+        nc.vector.memset(bias_row[:], 0.0)
+        first_sqrt = const.tile([P, 1], F32, name="first_sqrt")
+        nc.scalar.sqrt(out=first_sqrt[:], in_=one_col[:])
+        ones_b = const.tile([P, P], BF16, name="ones_b")
+        nc.vector.memset(ones_b[:], 1.0)
+        ident_b = const.tile([P, P], BF16, name="ident_b")
+        nc.vector.tensor_copy(out=ident_b[:], in_=ident_f[:])
+        row_in_group = const.tile([P, SLICES], F32, name="row_in_group")
+        nc.vector.tensor_reduce(
+            out=row_in_group[:],
+            in_=ident_f[:].rearrange("p (q t) -> p t q", t=SLICES),
+            axis=AX.X,
+            op=ALU.add,
+        )
+        group_of_row = const.tile([P, SPREAD], F32, name="group_of_row")
+        nc.vector.tensor_reduce(
+            out=group_of_row[:],
+            in_=ident_f[:].rearrange("p (q t) -> p q t", t=SLICES),
+            axis=AX.X,
+            op=ALU.add,
+        )
+        bias_all = const.tile([P, OUTF], F32, name="bias_all")
+        w_raw = const.tile([P, PASSES, PACK, OUTF], BF16, name="w_raw")
+        w_grouped = const.tile([P, PASSES, OUTF, PACK], BF16, name="w_grouped", align_bytes=64)
+        w_words = const.tile([P, PASSES, OUTF], U32, name="w_words", align_bytes=64)
+        w_scales = const.tile([P, PASSES, OUTF], U8, name="w_scales", align_bytes=64)
+        bias_bank = psum_o.tile([P, OUTF], F32, name="bias_bank", tag="o")
+
+        def load_mask(g, first_chunk, end_chunk):
+            if g not in mask_tiles:
+                mask_tiles[g] = mask_pool.tile(
+                    [P, CHUNKS, CHUNK_ROWS, NODES], BF16, name="mask%d" % g, tag="mask"
+                )
+            for c in range(first_chunk, end_chunk):
+                nc.sync.dma_start(out=mask_tiles[g][:, c], in_=mask_view[g][:, c])
+
+        def load_x(g, first_slice, end_slice):
+            if g not in x_tiles:
+                x_tiles[g] = x_pool.tile([P, SLICES, FEAT], BF16, name="x%d" % g, tag="x")
+            rows = slice(first_slice, end_slice)
+            nc.sync.dma_start(out=x_tiles[g][:, rows, :], in_=x_view[g][:, rows, :])
+
+        def self_loops(g):
+            width = P * CHUNK_ROWS
+            for c in range(CHUNKS):
+                for t in range(CHUNK_ROWS):
+                    region = mask_tiles[g][:, c, t, c * width : (c + 1) * width]
+                    nc.gpsimd.affine_select(
+                        out=region,
+                        in_=region,
+                        pattern=[[-1, width]],
+                        compare_op=ALU.not_equal,
+                        fill=LOOP,
+                        base=t,
+                        channel_multiplier=CHUNK_ROWS,
+                    )
+
+        def column_sums(g, c):
+            if c == 0:
+                sum_banks[g] = psum_d.tile(
+                    [P, CHUNKS, BLOCKS, SUM_COLS], F32, name="sums%d" % g, tag="d"
+                )
+            with_diagonal = [CHUNK_ROWS * c + t for t in range(CHUNK_ROWS)]
+            for b in [b for b in range(BLOCKS) if b not in with_diagonal] + with_diagonal:
+                for t in range(CHUNK_ROWS):
+                    nc.tensor.matmul(
+                        out=sum_banks[g][:, c, b, :],
+                        lhsT=mask_tiles[g][:, c, t, b * P : (b + 1) * P],
+                        rhs=ones_b[:, 0:SUM_COLS],
+                        start=(t == 0),
+                        stop=(t == CHUNK_ROWS - 1),
+                    )
+
+        def degree_spread(g):
+            d_block = small.tile([P, BLOCKS], F32, name="d_block%d" % g, tag="d_block")
+            nc.vector.tensor_reduce(
+                out=d_block[:],
+                in_=sum_banks[g][:].rearrange("p c b n -> p b c n")[:, :, :, 0],
+                axis=AX.X,
+                op=ALU.add,
+            )
+            spread_tiles[g] = small.tile([P, BLOCKS, SPREAD], F32, name="spread%d" % g, tag="spread")
+            nc.vector.tensor_tensor(
+                out=spread_tiles[g][:],
+                in0=d_block[:].unsqueeze(2).to_broadcast([P, BLOCKS, SPREAD]),
+                in1=group_of_row[:].unsqueeze(1).to_broadcast([P, BLOCKS, SPREAD]),
+                op=ALU.mult,
+            )
+
+        def degree_resort(g):
+            nc.tensor.matmul(
+                out=sum_banks[g][:, 0, 0, 0:SLICES],
+                lhsT=spread_tiles[g][:].rearrange("p b q -> p (b q)"),
+                rhs=row_in_group[:],
+                start=True,
+                stop=True,
+            )
+
+        def degree_root(g):
+            root_tiles[g] = small.tile([P, SLICES], F32, name="root%d" % g, tag="root")
+            nc.scalar.sqrt(out=root_tiles[g][:], in_=sum_banks[g][:, 0, 0, 0:SLICES])
+
+        def degree_reciprocal(g):
+            inv_sqrt_d[g] = small.tile([P, SLICES], F32, name="inv_sqrt_d%d" % g, tag="inv_sqrt_d")
+            nc.vector.reciprocal(out=inv_sqrt_d[g][:], in_=root_tiles[g][:])
+
+        def bias_matmul(times):
+            for repeat in range(times):
+                nc.tensor.matmul(
+                    out=bias_bank[:], lhsT=ones_b[:], rhs=bias_row[:], start=True, stop=True
+                )
+
+        def weight_group(c):
+            nc.vector.tensor_copy(
+                out=w_grouped[:, c].rearrange("p (a i) t -> p a t i", i=4),
+                in_=w_raw[:, c].rearrange("p t (a i) -> p a t i", i=4),
+            )
+
+        def scale_rows(r):
+            g, q = divmod(r, ROUNDS_PER_GRAPH)
+            scaled[r] = work.tile([P, PAIR, FEAT], BF16, name="scaled%d" % r, tag="scaled")
+            for s in range(PAIR):
+                t = PAIR * q + s
+                nc.vector.tensor_scalar(
+                    out=scaled[r][:, s, :],
+                    in0=x_tiles[g][:, t, :],
+                    scalar1=inv_sqrt_d[g][:, t : t + 1],
+                    scalar2=None,
+                    op0=ALU.mult,
+                )
+
+        def transpose_slice(r, s):
+            bank = psum_t.tile([P, BLOCKS, P], BF16, name="flipped%d_%d" % (r, s), tag="t")
+            flipped[(r, s)] = bank
+            for b in range(BLOCKS):
+                c, t = divmod(b, PACK)
+                columns = slice(c * P * PACK + t, (c + 1) * P * PACK, PACK)
+                nc.tensor.transpose(bank[:, b, :], scaled[r][:, s, columns], ident_b[:])
+
+        def group_slice(r, s):
+            if s == 0:
+                grouped[r] = work.tile(
+                    [P, PAIR, PASSES, P, PACK], BF16, name="grouped%d" % r, tag="grouped", align_bytes=64
+                )
+            nc.scalar.copy(
+                out=grouped[r][:, s],
+                in_=flipped[(r, s)][:].rearrange("p (c t) i -> p c i t", c=PASSES),
+            )
+
+        def quantise(r):
+            width = PASSES * P
+            words = work.tile([P, PAIR * width], U32, name="words%d" % r, tag="words", align_bytes=64)
+            scales = work.tile([P, PAIR * width], U8, name="scales%d" % r, tag="scales", align_bytes=64)
+            packed[r] = (words, scales)
+            if r == ROUNDS - 1:
+                for s in range(PAIR):
+                    cols = slice(s * width, (s + 1) * width)
+                    nc.vector.quantize_mx(
+                        out=words[:, cols].bitcast(FP8X4),
+                        scales=scales[:, cols],
+                        in_=grouped[r][:, s].rearrange("p c i t -> p (c i t)"),
+                    )
+            else:
+                nc.vector.quantize_mx(
+                    out=words[:].bitcast(FP8X4),
+                    scales=scales[:],
+                    in_=grouped[r][:].rearrange("p s c i t -> p (s c i t)"),
+                )
+
+        def multiply_slice(r, s):
+            words, scales = packed[r]
+            bank = psum_o.tile([P, OUTF], F32, name="product%d_%d" % (r, s), tag="o")
+            products[(r, s)] = bank
+            for c in range(PASSES):
+                cols = slice((PASSES * s + c) * P, (PASSES * s + c + 1) * P)
+                nc.tensor.matmul_mx(
+                    out=bank[:],
+                    lhsT=words[:, cols].bitcast(FP8X4),
+                    lhsT_scale=scales[:, cols],
+                    rhs=w_words[:, c, :].bitcast(FP8X4),
+                    rhs_scale=w_scales[:, c, :],
+                    start=(c == 0),
+                    stop=(c == PASSES - 1),
+                )
+
+        def add_bias(r):
+            results[r] = result_pool.tile([P, PAIR, OUTF], F32, name="result%d" % r, tag="result")
+            for s in range(PAIR):
+                nc.vector.tensor_tensor(
+                    out=results[r][:, s, :], in0=products[(r, s)][:], in1=bias_all[:], op=ALU.add
+                )
+
+        def relu_slice(r, s, engine):
+            part = results[r][:, s, :]
+            if engine == "scalar":
+                nc.scalar.activation(out=part, in_=part, func=ACT.Relu)
+            else:
+                nc.vector.tensor_scalar_max(out=part, in0=part, scalar1=0.0)
+
+        def store(r, first_slice, end_slice):
+            g, q = divmod(r, ROUNDS_PER_GRAPH)
+            nc.sync.dma_start(
+                out=out_view[g][:, PAIR * q + first_slice : PAIR * q + end_slice, :],
+                in_=results[r][:, first_slice:end_slice, :],
+            )
+
+        load_mask(0, 0, 2)
+        nc.sync.dma_start(out=bias_row[0:1, :], in_=bias_view)
+        load_mask(0, 2, 4)
+        nc.sync.dma_start(out=w_raw[:], in_=weight_view)
+        load_x(0, 0, 2)
+        load_x(0, 2, 4)
+        load_mask(1, 0, 2)
+        load_x(0, 4, 6)
+        load_mask(1, 2, 4)
+        load_x(0, 6, 8)
+        load_x(1, 0, 2)
+        load_x(1, 2, 4)
+        load_mask(2, 0, 2)
+        load_x(1, 4, 8)
+        load_mask(2, 2, 4)
+        load_x(2, 0, 4)
+        load_x(2, 4, 8)
+        for g in range(RESIDENT):
+            self_loops(g)
+
+        column_sums(0, 0)
+        column_sums(0, 1)
+        bias_matmul(1)
+        nc.scalar.copy(out=bias_all[:], in_=bias_bank[:])
+        column_sums(0, 2)
+        column_sums(0, 3)
+        bias_matmul(CLOCK_REPEATS)
+        load_mask(3, 0, 4)
+        self_loops(3)
+        degree_spread(0)
+        degree_resort(0)
+        bias_matmul(CLOCK_REPEATS)
+        degree_root(0)
+        weight_group(0)
+        degree_reciprocal(0)
+        for r in range(LEAD):
+            scale_rows(r)
+            transpose_slice(r, 0)
+            bias_matmul(CLOCK_REPEATS)
+            transpose_slice(r, 1)
+            group_slice(r, 0)
+            group_slice(r, 1)
+            if r == 0:
+                weight_group(1)
+        nc.vector.quantize_mx(
+            out=w_words[:].rearrange("p c o -> p (c o)").bitcast(FP8X4),
+            scales=w_scales[:].rearrange("p c o -> p (c o)"),
+            in_=w_grouped[:].rearrange("p c o t -> p (c o t)"),
+        )
+        column_sums(1, 0)
+        column_sums(1, 1)
+        bias_matmul(CLOCK_REPEATS)
+
+        def sums_due(r, s):
+            if r == 0:
+                return [(1, PAIR + s)]
+            g, k = divmod(r + LEAD, ROUNDS_PER_GRAPH)
+            if k < LEAD and g + 1 < GRAPHS:
+                return [(g + 1, PAIR * k + s)]
+            return []
+
+        for r in range(ROUNDS + 1):
+            ahead = r + LEAD
+            behind = r - 1
+            next_graph = r // ROUNDS_PER_GRAPH + 1
+            degrees_now = r % ROUNDS_PER_GRAPH == 1 and next_graph < GRAPHS
+
+            if ahead < ROUNDS:
+                scale_rows(ahead)
+                if ahead == ROUNDS_PER_GRAPH - 1:
+                    load_x(3, 0, 4)
+                    load_x(3, 4, 8)
+            if r < ROUNDS:
+                quantise(r)
+            if degrees_now:
+                degree_spread(next_graph)
+            for s in range(PAIR):
+                if ahead < ROUNDS:
+                    transpose_slice(ahead, s)
+                if r < ROUNDS:
+                    multiply_slice(r, s)
+                for g, c in sums_due(r, s):
+                    column_sums(g, c)
+                if degrees_now and s == 0:
+                    degree_resort(next_graph)
+            if behind >= 0:
+                add_bias(behind)
+            last_copies = ahead == ROUNDS - 1
+            if ahead < ROUNDS:
+                group_slice(ahead, 0)
+            if degrees_now:
+                degree_root(next_graph)
+            if behind >= 0 and not last_copies:
+                relu_slice(behind, 0, "scalar")
+            if ahead < ROUNDS:
+                group_slice(ahead, 1)
+            if behind >= 0 and last_copies:
+                relu_slice(behind, 0, "scalar")
+            if behind == ROUNDS - 1:
+                store(behind, 0, 1)
+                relu_slice(behind, 1, "vector")
+                store(behind, 1, 2)
+            elif behind >= 0:
+                relu_slice(behind, 1, "scalar" if ahead >= ROUNDS else "vector")
+                store(behind, 0, PAIR)
+            if degrees_now:
+                degree_reciprocal(next_graph)

@@ -19,7 +19,9 @@ NODES = 1024
 FEAT = 1024
 OUTF = 512
 PASSES = FEAT // (P * PACK)
-BLOCKS = FEAT // P
+BLOCKS = NODES // P
+HALVES = 2
+PAIR_COLS = FEAT // 2 // HALVES
 SLICES = NODES // P
 PAIR = 2
 ROUNDS_PER_GRAPH = SLICES // PAIR
@@ -79,8 +81,6 @@ def tile_gcn_t_kernel(tc, x, mask, weight, bias, out):
         nc.scalar.sqrt(out=first_sqrt[:], in_=one_col[:])
         ones_b = const.tile([P, P], BF16, name="ones_b")
         nc.vector.memset(ones_b[:], 1.0)
-        ident_b = const.tile([P, P], BF16, name="ident_b")
-        nc.vector.tensor_copy(out=ident_b[:], in_=ident_f[:])
         row_in_group = const.tile([P, SLICES], F32, name="row_in_group")
         nc.vector.tensor_reduce(
             out=row_in_group[:],
@@ -194,24 +194,25 @@ def tile_gcn_t_kernel(tc, x, mask, weight, bias, out):
 
         def scale_rows(r):
             g, q = divmod(r, ROUNDS_PER_GRAPH)
-            scaled[r] = work.tile([P, PAIR, FEAT], BF16, name="scaled%d" % r, tag="scaled")
+            scaled[r] = work.tile([P, PAIR, HALVES, PAIR_COLS, 2], BF16, name="scaled%d" % r, tag="scaled")
             for s in range(PAIR):
                 t = PAIR * q + s
                 nc.vector.tensor_scalar(
-                    out=scaled[r][:, s, :],
-                    in0=x_tiles[g][:, t, :],
+                    out=scaled[r][:, s],
+                    in0=x_tiles[g][:, t, :].rearrange("p (m u e) -> p u m e", u=HALVES, e=2),
                     scalar1=inv_sqrt_d[g][:, t : t + 1],
                     scalar2=None,
                     op0=ALU.mult,
                 )
 
         def transpose_slice(r, s):
-            bank = psum_t.tile([P, BLOCKS, P], BF16, name="flipped%d_%d" % (r, s), tag="t")
+            bank = psum_t.tile([P, PASSES, HALVES, P], F32, name="flipped%d_%d" % (r, s), tag="t")
             flipped[(r, s)] = bank
-            for b in range(BLOCKS):
-                c, t = divmod(b, PACK)
-                columns = slice(c * P * PACK + t, (c + 1) * P * PACK, PACK)
-                nc.tensor.transpose(bank[:, b, :], scaled[r][:, s, columns], ident_b[:])
+            pairs = scaled[r][:, s].rearrange("p u m e -> p (u m e)").bitcast(F32)
+            for c in range(PASSES):
+                for u in range(HALVES):
+                    first = u * PAIR_COLS + c * P
+                    nc.tensor.transpose(bank[:, c, u, :], pairs[:, first : first + P], ident_f[:])
 
         def group_slice(r, s):
             if s == 0:
@@ -219,8 +220,11 @@ def tile_gcn_t_kernel(tc, x, mask, weight, bias, out):
                     [P, PAIR, PASSES, P, PACK], BF16, name="grouped%d" % r, tag="grouped", align_bytes=64
                 )
             nc.scalar.copy(
-                out=grouped[r][:, s],
-                in_=flipped[(r, s)][:].rearrange("p (c t) i -> p c i t", c=PASSES),
+                out=grouped[r][:, s]
+                .rearrange("p c i t -> p (c i t)")
+                .bitcast(F32)
+                .rearrange("p (c i u) -> p c i u", c=PASSES, u=HALVES),
+                in_=flipped[(r, s)][:].rearrange("p c u i -> p c i u"),
             )
 
         def quantise(r):

@@ -29,9 +29,9 @@ ROUNDS = GRAPHS * ROUNDS_PER_GRAPH
 LEAD = 2
 CHUNKS = 4
 CHUNK_ROWS = 2
-SUM_COLS = 16
+SUM_SLOT = 14
+SUM_COLS = 32
 SPREAD = P // SLICES
-CLOCK_REPEATS = 2
 RESIDENT = 3
 RESULT_BUFS = 12
 LOOP = 1.0
@@ -71,16 +71,31 @@ def tile_gcn_t_kernel(tc, x, mask, weight, bias, out):
         products = {}
         results = {}
 
+        def clear_diagonal(region, t):
+            nc.gpsimd.affine_select(
+                out=region,
+                in_=region,
+                pattern=[[-1, P * CHUNK_ROWS]],
+                compare_op=ALU.not_equal,
+                fill=0.0,
+                base=t,
+                channel_multiplier=CHUNK_ROWS,
+            )
+
         ident_f = const.tile([P, P], F32, name="ident_f")
-        make_identity(nc, ident_f[:])
         one_col = const.tile([P, 1], F32, name="one_col")
         nc.vector.memset(one_col[:], 1.0)
+        ones_b = const.tile([P, OUTF], BF16, name="ones_b")
+        nc.vector.memset(ones_b[:], 1.0)
         bias_row = const.tile([P, OUTF], BF16, name="bias_row")
         nc.vector.memset(bias_row[:], 0.0)
         first_sqrt = const.tile([P, 1], F32, name="first_sqrt")
         nc.scalar.sqrt(out=first_sqrt[:], in_=one_col[:])
-        ones_b = const.tile([P, P], BF16, name="ones_b")
-        nc.vector.memset(ones_b[:], 1.0)
+        make_identity(nc, ident_f[:])
+        off_diagonal = const.tile([P, CHUNK_ROWS, P * CHUNK_ROWS], BF16, name="off_diagonal")
+        nc.gpsimd.memset(off_diagonal[:], 1.0)
+        for t in range(CHUNK_ROWS):
+            clear_diagonal(off_diagonal[:, t, :], t)
         row_in_group = const.tile([P, SLICES], F32, name="row_in_group")
         nc.vector.tensor_reduce(
             out=row_in_group[:],
@@ -116,33 +131,31 @@ def tile_gcn_t_kernel(tc, x, mask, weight, bias, out):
             rows = slice(first_slice, end_slice)
             nc.sync.dma_start(out=x_tiles[g][:, rows, :], in_=x_view[g][:, rows, :])
 
-        def self_loops(g):
+        def diagonal_of(g, c):
             width = P * CHUNK_ROWS
+            return mask_tiles[g][:, c, :, c * width : (c + 1) * width]
+
+        def clear_diagonals(g):
             for c in range(CHUNKS):
                 for t in range(CHUNK_ROWS):
-                    region = mask_tiles[g][:, c, t, c * width : (c + 1) * width]
-                    nc.gpsimd.affine_select(
-                        out=region,
-                        in_=region,
-                        pattern=[[-1, width]],
-                        compare_op=ALU.not_equal,
-                        fill=LOOP,
-                        base=t,
-                        channel_multiplier=CHUNK_ROWS,
-                    )
+                    clear_diagonal(diagonal_of(g, c)[:, t, :], t)
+
+        def mask_diagonal(g, c):
+            region = diagonal_of(g, c)
+            nc.vector.tensor_tensor(out=region, in0=region, in1=off_diagonal[:], op=ALU.mult)
 
         def column_sums(g, c):
             if c == 0:
-                sum_banks[g] = psum_d.tile(
-                    [P, CHUNKS, BLOCKS, SUM_COLS], F32, name="sums%d" % g, tag="d"
-                )
+                sum_banks[g] = psum_d.tile([P, OUTF], F32, name="sums%d" % g, tag="d")
             with_diagonal = [CHUNK_ROWS * c + t for t in range(CHUNK_ROWS)]
             for b in [b for b in range(BLOCKS) if b not in with_diagonal] + with_diagonal:
+                first = (BLOCKS * c + b) * SUM_SLOT
+                width = SUM_SLOT if b in with_diagonal else SUM_COLS
                 for t in range(CHUNK_ROWS):
                     nc.tensor.matmul(
-                        out=sum_banks[g][:, c, b, :],
+                        out=sum_banks[g][:, first : first + width],
                         lhsT=mask_tiles[g][:, c, t, b * P : (b + 1) * P],
-                        rhs=ones_b[:, 0:SUM_COLS],
+                        rhs=ones_b[:, 0:width],
                         start=(t == 0),
                         stop=(t == CHUNK_ROWS - 1),
                     )
@@ -151,21 +164,25 @@ def tile_gcn_t_kernel(tc, x, mask, weight, bias, out):
             d_block = small.tile([P, BLOCKS], F32, name="d_block%d" % g, tag="d_block")
             nc.vector.tensor_reduce(
                 out=d_block[:],
-                in_=sum_banks[g][:].rearrange("p c b n -> p b c n")[:, :, :, 0],
+                in_=sum_banks[g][:, 0 : CHUNKS * BLOCKS * SUM_SLOT].rearrange(
+                    "p (c b n) -> p b c n", c=CHUNKS, n=SUM_SLOT
+                )[:, :, :, 0],
                 axis=AX.X,
                 op=ALU.add,
             )
             spread_tiles[g] = small.tile([P, BLOCKS, SPREAD], F32, name="spread%d" % g, tag="spread")
-            nc.vector.tensor_tensor(
+            nc.vector.scalar_tensor_tensor(
                 out=spread_tiles[g][:],
                 in0=d_block[:].unsqueeze(2).to_broadcast([P, BLOCKS, SPREAD]),
+                scalar=LOOP,
                 in1=group_of_row[:].unsqueeze(1).to_broadcast([P, BLOCKS, SPREAD]),
-                op=ALU.mult,
+                op0=ALU.add,
+                op1=ALU.mult,
             )
 
         def degree_resort(g):
             nc.tensor.matmul(
-                out=sum_banks[g][:, 0, 0, 0:SLICES],
+                out=sum_banks[g][:, 0:SLICES],
                 lhsT=spread_tiles[g][:].rearrange("p b q -> p (b q)"),
                 rhs=row_in_group[:],
                 start=True,
@@ -174,22 +191,29 @@ def tile_gcn_t_kernel(tc, x, mask, weight, bias, out):
 
         def degree_root(g):
             root_tiles[g] = small.tile([P, SLICES], F32, name="root%d" % g, tag="root")
-            nc.scalar.sqrt(out=root_tiles[g][:], in_=sum_banks[g][:, 0, 0, 0:SLICES])
+            nc.scalar.sqrt(out=root_tiles[g][:], in_=sum_banks[g][:, 0:SLICES])
 
         def degree_reciprocal(g):
             inv_sqrt_d[g] = small.tile([P, SLICES], F32, name="inv_sqrt_d%d" % g, tag="inv_sqrt_d")
             nc.vector.reciprocal(out=inv_sqrt_d[g][:], in_=root_tiles[g][:])
 
-        def bias_matmul(times):
-            for repeat in range(times):
-                nc.tensor.matmul(
-                    out=bias_bank[:], lhsT=ones_b[:], rhs=bias_row[:], start=True, stop=True
-                )
+        def bias_matmul():
+            nc.tensor.matmul(out=bias_bank[:], lhsT=ones_b[:, 0:P], rhs=bias_row[:], start=True, stop=True)
 
-        def weight_group(c):
-            nc.vector.tensor_copy(
+        def warm_clock(columns):
+            nc.tensor.matmul(out=bias_bank[:], lhsT=ones_b[:, 0:P], rhs=columns, start=True, stop=True)
+
+        def weight_group(c, copy):
+            copy(
                 out=w_grouped[:, c].rearrange("p (a i) t -> p a t i", i=4),
                 in_=w_raw[:, c].rearrange("p t (a i) -> p a t i", i=4),
+            )
+
+        def weight_quantise(c):
+            nc.vector.quantize_mx(
+                out=w_words[:, c, :].bitcast(FP8X4),
+                scales=w_scales[:, c, :],
+                in_=w_grouped[:, c].rearrange("p o t -> p (o t)"),
             )
 
         def scale_rows(r):
@@ -232,7 +256,7 @@ def tile_gcn_t_kernel(tc, x, mask, weight, bias, out):
             words = work.tile([P, PAIR * width], U32, name="words%d" % r, tag="words", align_bytes=64)
             scales = work.tile([P, PAIR * width], U8, name="scales%d" % r, tag="scales", align_bytes=64)
             packed[r] = (words, scales)
-            if r == ROUNDS - 1:
+            if r in (0, ROUNDS - 1):
                 for s in range(PAIR):
                     cols = slice(s * width, (s + 1) * width)
                     nc.vector.quantize_mx(
@@ -284,110 +308,115 @@ def tile_gcn_t_kernel(tc, x, mask, weight, bias, out):
                 in_=results[r][:, first_slice:end_slice, :],
             )
 
-        load_mask(0, 0, 2)
-        nc.sync.dma_start(out=bias_row[0:1, :], in_=bias_view)
-        load_mask(0, 2, 4)
-        nc.sync.dma_start(out=w_raw[:], in_=weight_view)
-        load_x(0, 0, 2)
-        load_x(0, 2, 4)
-        load_mask(1, 0, 2)
-        load_x(0, 4, 6)
-        load_mask(1, 2, 4)
-        load_x(0, 6, 8)
-        load_x(1, 0, 2)
-        load_x(1, 2, 4)
-        load_mask(2, 0, 2)
-        load_x(1, 4, 8)
-        load_mask(2, 2, 4)
-        load_x(2, 0, 4)
-        load_x(2, 4, 8)
-        for g in range(RESIDENT):
-            self_loops(g)
+        def prepare(r):
+            scale_rows(r)
+            for s in range(PAIR):
+                transpose_slice(r, s)
+            for s in range(PAIR):
+                group_slice(r, s)
 
-        column_sums(0, 0)
-        column_sums(0, 1)
-        bias_matmul(1)
-        nc.scalar.copy(out=bias_all[:], in_=bias_bank[:])
-        column_sums(0, 2)
-        column_sums(0, 3)
-        bias_matmul(CLOCK_REPEATS)
-        load_mask(3, 0, 4)
-        self_loops(3)
+        for c in range(PASSES):
+            nc.sync.dma_start(out=w_raw[:, c], in_=weight_view[:, c])
+        load_mask(0, 0, CHUNKS)
+        load_x(0, 0, PAIR)
+        nc.sync.dma_start(out=bias_row[0:1, :], in_=bias_view)
+        load_mask(1, 0, 1)
+        for c in range(1, CHUNKS):
+            load_x(0, PAIR * c, PAIR * c + PAIR)
+            load_mask(1, c, c + 1)
+        for c in range(CHUNKS):
+            load_mask(2, c, c + 1)
+            load_x(1, PAIR * c, PAIR * c + PAIR)
+        for g in range(1, RESIDENT):
+            clear_diagonals(g)
+
+        for c in range(PASSES):
+            warm_clock(w_raw[:, c, 0, :])
+            warm_clock(w_raw[:, c, 1, :])
+        weight_group(0, nc.vector.tensor_copy)
+        weight_group(1, nc.scalar.copy)
+        weight_quantise(0)
+        for c in range(CHUNKS):
+            mask_diagonal(0, c)
+            if c == 1:
+                weight_quantise(1)
+            if c > 0:
+                warm_clock(ones_b[:])
+            column_sums(0, c)
+        for c in range(CHUNKS):
+            load_mask(3, c, c + 1)
+            load_x(2, PAIR * c, PAIR * c + PAIR)
+        clear_diagonals(3)
         degree_spread(0)
         degree_resort(0)
-        bias_matmul(CLOCK_REPEATS)
+        warm_clock(ones_b[:])
+        warm_clock(ones_b[:])
         degree_root(0)
-        weight_group(0)
         degree_reciprocal(0)
-        for r in range(LEAD):
-            scale_rows(r)
-            transpose_slice(r, 0)
-            bias_matmul(CLOCK_REPEATS)
-            transpose_slice(r, 1)
-            group_slice(r, 0)
-            group_slice(r, 1)
-            if r == 0:
-                weight_group(1)
-        nc.vector.quantize_mx(
-            out=w_words[:].rearrange("p c o -> p (c o)").bitcast(FP8X4),
-            scales=w_scales[:].rearrange("p c o -> p (c o)"),
-            in_=w_grouped[:].rearrange("p c o t -> p (c o t)"),
-        )
+        prepare(0)
+        bias_matmul()
+        nc.scalar.copy(out=bias_all[:], in_=bias_bank[:])
         column_sums(1, 0)
-        column_sums(1, 1)
-        bias_matmul(CLOCK_REPEATS)
 
-        def sums_due(r, s):
+        def sums_due(r):
             if r == 0:
-                return [(1, PAIR + s)]
-            g, k = divmod(r + LEAD, ROUNDS_PER_GRAPH)
-            if k < LEAD and g + 1 < GRAPHS:
-                return [(g + 1, PAIR * k + s)]
-            return []
+                return [(1, 1), (1, 2)]
+            g, c = divmod(r + 2 * ROUNDS_PER_GRAPH - 1, ROUNDS_PER_GRAPH)
+            return ([(1, 3)] if r == 1 else []) + ([(g, c)] if g < GRAPHS else [])
 
         for r in range(ROUNDS + 1):
             ahead = r + LEAD
             behind = r - 1
             next_graph = r // ROUNDS_PER_GRAPH + 1
-            degrees_now = r % ROUNDS_PER_GRAPH == 1 and next_graph < GRAPHS
+            finishing = r % ROUNDS_PER_GRAPH == LEAD - 1 and next_graph < GRAPHS
+            first_use = r % ROUNDS_PER_GRAPH == LEAD and next_graph < GRAPHS
+            due = sums_due(r)
 
+            if r < ROUNDS:
+                quantise(r)
+                for s in range(PAIR):
+                    multiply_slice(r, s)
+            if r == 0:
+                for a in range(1, LEAD + 1):
+                    prepare(a)
+                for g, c in due:
+                    column_sums(g, c)
+                continue
+            if first_use:
+                add_bias(behind)
+                degree_reciprocal(next_graph)
+            if r == 1 or first_use:
+                for g, c in due[:1]:
+                    column_sums(g, c)
+                due = due[1:]
             if ahead < ROUNDS:
                 scale_rows(ahead)
+                for s in range(PAIR):
+                    transpose_slice(ahead, s)
                 if ahead == ROUNDS_PER_GRAPH - 1:
                     load_x(3, 0, 4)
                     load_x(3, 4, 8)
-            if r < ROUNDS:
-                quantise(r)
-            if degrees_now:
-                degree_spread(next_graph)
-            for s in range(PAIR):
-                if ahead < ROUNDS:
-                    transpose_slice(ahead, s)
-                if r < ROUNDS:
-                    multiply_slice(r, s)
-                for g, c in sums_due(r, s):
-                    column_sums(g, c)
-                if degrees_now and s == 0:
-                    degree_resort(next_graph)
-            if behind >= 0:
+            if not first_use:
                 add_bias(behind)
-            last_copies = ahead == ROUNDS - 1
+            if finishing:
+                degree_spread(next_graph)
+                degree_resort(next_graph)
+            for g, c in due:
+                column_sums(g, c)
             if ahead < ROUNDS:
                 group_slice(ahead, 0)
-            if degrees_now:
-                degree_root(next_graph)
-            if behind >= 0 and not last_copies:
+            if ahead != ROUNDS - 1:
                 relu_slice(behind, 0, "scalar")
             if ahead < ROUNDS:
                 group_slice(ahead, 1)
-            if behind >= 0 and last_copies:
+            if ahead == ROUNDS - 1:
                 relu_slice(behind, 0, "scalar")
+            if finishing:
+                degree_root(next_graph)
             if behind == ROUNDS - 1:
                 store(behind, 0, 1)
                 relu_slice(behind, 1, "vector")
                 store(behind, 1, 2)
-            elif behind >= 0:
-                relu_slice(behind, 1, "scalar" if ahead >= ROUNDS else "vector")
+            else:
+                relu_slice(behind, 1, "scalar")
                 store(behind, 0, PAIR)
-            if degrees_now:
-                degree_reciprocal(next_graph)

@@ -62,6 +62,7 @@ def tile_gcn_t_kernel(tc, x, mask, weight, bias, out):
         x_tiles = {}
         sum_banks = {}
         spread_tiles = {}
+        sorted_degrees = {}
         root_tiles = {}
         inv_sqrt_d = {}
         scaled = {}
@@ -181,8 +182,9 @@ def tile_gcn_t_kernel(tc, x, mask, weight, bias, out):
             )
 
         def degree_resort(g):
+            sorted_degrees[g] = psum_t.tile([P, SLICES], F32, name="sorted%d" % g, tag="t")
             nc.tensor.matmul(
-                out=sum_banks[g][:, 0:SLICES],
+                out=sorted_degrees[g][:],
                 lhsT=spread_tiles[g][:].rearrange("p b q -> p (b q)"),
                 rhs=row_in_group[:],
                 start=True,
@@ -191,7 +193,7 @@ def tile_gcn_t_kernel(tc, x, mask, weight, bias, out):
 
         def degree_root(g):
             root_tiles[g] = small.tile([P, SLICES], F32, name="root%d" % g, tag="root")
-            nc.scalar.sqrt(out=root_tiles[g][:], in_=sum_banks[g][:, 0:SLICES])
+            nc.scalar.sqrt(out=root_tiles[g][:], in_=sorted_degrees[g][:])
 
         def degree_reciprocal(g):
             inv_sqrt_d[g] = small.tile([P, SLICES], F32, name="inv_sqrt_d%d" % g, tag="inv_sqrt_d")
@@ -359,10 +361,8 @@ def tile_gcn_t_kernel(tc, x, mask, weight, bias, out):
         column_sums(1, 0)
 
         def sums_due(r):
-            if r == 0:
-                return [(1, 1), (1, 2)]
-            g, c = divmod(r + 2 * ROUNDS_PER_GRAPH - 1, ROUNDS_PER_GRAPH)
-            return ([(1, 3)] if r == 1 else []) + ([(g, c)] if g < GRAPHS else [])
+            g, c = divmod(r + ROUNDS_PER_GRAPH + LEAD, ROUNDS_PER_GRAPH)
+            return ([(1, 1)] if r == 0 else []) + ([(g, c)] if g < GRAPHS else [])
 
         for r in range(ROUNDS + 1):
             ahead = r + LEAD
@@ -370,7 +370,6 @@ def tile_gcn_t_kernel(tc, x, mask, weight, bias, out):
             next_graph = r // ROUNDS_PER_GRAPH + 1
             finishing = r % ROUNDS_PER_GRAPH == LEAD - 1 and next_graph < GRAPHS
             first_use = r % ROUNDS_PER_GRAPH == LEAD and next_graph < GRAPHS
-            due = sums_due(r)
 
             if r < ROUNDS:
                 quantise(r)
@@ -379,16 +378,13 @@ def tile_gcn_t_kernel(tc, x, mask, weight, bias, out):
             if r == 0:
                 for a in range(1, LEAD + 1):
                     prepare(a)
-                for g, c in due:
-                    column_sums(g, c)
+            for g, c in sums_due(r):
+                column_sums(g, c)
+            if r == 0:
                 continue
             if first_use:
                 add_bias(behind)
                 degree_reciprocal(next_graph)
-            if r == 1 or first_use:
-                for g, c in due[:1]:
-                    column_sums(g, c)
-                due = due[1:]
             if ahead < ROUNDS:
                 scale_rows(ahead)
                 for s in range(PAIR):
@@ -401,8 +397,6 @@ def tile_gcn_t_kernel(tc, x, mask, weight, bias, out):
             if finishing:
                 degree_spread(next_graph)
                 degree_resort(next_graph)
-            for g, c in due:
-                column_sums(g, c)
             if ahead < ROUNDS:
                 group_slice(ahead, 0)
             if ahead != ROUNDS - 1:

@@ -63,7 +63,6 @@ def tile_gcn_t_kernel(tc, x, mask, weight, bias, out):
         sum_banks = {}
         spread_tiles = {}
         sorted_degrees = {}
-        root_tiles = {}
         inv_sqrt_d = {}
         scaled = {}
         flipped = {}
@@ -72,17 +71,6 @@ def tile_gcn_t_kernel(tc, x, mask, weight, bias, out):
         products = {}
         results = {}
 
-        def clear_diagonal(region, t):
-            nc.gpsimd.affine_select(
-                out=region,
-                in_=region,
-                pattern=[[-1, P * CHUNK_ROWS]],
-                compare_op=ALU.not_equal,
-                fill=0.0,
-                base=t,
-                channel_multiplier=CHUNK_ROWS,
-            )
-
         ident_f = const.tile([P, P], F32, name="ident_f")
         one_col = const.tile([P, 1], F32, name="one_col")
         nc.vector.memset(one_col[:], 1.0)
@@ -90,13 +78,21 @@ def tile_gcn_t_kernel(tc, x, mask, weight, bias, out):
         nc.vector.memset(ones_b[:], 1.0)
         bias_row = const.tile([P, OUTF], BF16, name="bias_row")
         nc.vector.memset(bias_row[:], 0.0)
-        first_sqrt = const.tile([P, 1], F32, name="first_sqrt")
-        nc.scalar.sqrt(out=first_sqrt[:], in_=one_col[:])
+        first_root = const.tile([P, 1], F32, name="first_root")
+        nc.scalar.activation(out=first_root[:], in_=one_col[:], func=ACT.Abs_reciprocal_sqrt)
         make_identity(nc, ident_f[:])
         off_diagonal = const.tile([P, CHUNK_ROWS, P * CHUNK_ROWS], BF16, name="off_diagonal")
         nc.gpsimd.memset(off_diagonal[:], 1.0)
         for t in range(CHUNK_ROWS):
-            clear_diagonal(off_diagonal[:, t, :], t)
+            nc.gpsimd.affine_select(
+                out=off_diagonal[:, t, :],
+                in_=off_diagonal[:, t, :],
+                pattern=[[-1, P * CHUNK_ROWS]],
+                compare_op=ALU.not_equal,
+                fill=0.0,
+                base=t,
+                channel_multiplier=CHUNK_ROWS,
+            )
         row_in_group = const.tile([P, SLICES], F32, name="row_in_group")
         nc.vector.tensor_reduce(
             out=row_in_group[:],
@@ -132,17 +128,9 @@ def tile_gcn_t_kernel(tc, x, mask, weight, bias, out):
             rows = slice(first_slice, end_slice)
             nc.sync.dma_start(out=x_tiles[g][:, rows, :], in_=x_view[g][:, rows, :])
 
-        def diagonal_of(g, c):
-            width = P * CHUNK_ROWS
-            return mask_tiles[g][:, c, :, c * width : (c + 1) * width]
-
-        def clear_diagonals(g):
-            for c in range(CHUNKS):
-                for t in range(CHUNK_ROWS):
-                    clear_diagonal(diagonal_of(g, c)[:, t, :], t)
-
         def mask_diagonal(g, c):
-            region = diagonal_of(g, c)
+            width = P * CHUNK_ROWS
+            region = mask_tiles[g][:, c, :, c * width : (c + 1) * width]
             nc.vector.tensor_tensor(out=region, in0=region, in1=off_diagonal[:], op=ALU.mult)
 
         def column_sums(g, c):
@@ -191,13 +179,9 @@ def tile_gcn_t_kernel(tc, x, mask, weight, bias, out):
                 stop=True,
             )
 
-        def degree_root(g):
-            root_tiles[g] = small.tile([P, SLICES], F32, name="root%d" % g, tag="root")
-            nc.scalar.sqrt(out=root_tiles[g][:], in_=sorted_degrees[g][:])
-
-        def degree_reciprocal(g):
+        def degree_inverse_root(g):
             inv_sqrt_d[g] = small.tile([P, SLICES], F32, name="inv_sqrt_d%d" % g, tag="inv_sqrt_d")
-            nc.vector.reciprocal(out=inv_sqrt_d[g][:], in_=root_tiles[g][:])
+            nc.scalar.activation(out=inv_sqrt_d[g][:], in_=sorted_degrees[g][:], func=ACT.Abs_reciprocal_sqrt)
 
         def bias_matmul():
             nc.tensor.matmul(out=bias_bank[:], lhsT=ones_b[:, 0:P], rhs=bias_row[:], start=True, stop=True)
@@ -329,8 +313,6 @@ def tile_gcn_t_kernel(tc, x, mask, weight, bias, out):
         for c in range(CHUNKS):
             load_mask(2, c, c + 1)
             load_x(1, PAIR * c, PAIR * c + PAIR)
-        for g in range(1, RESIDENT):
-            clear_diagonals(g)
 
         for c in range(PASSES):
             warm_clock(w_raw[:, c, 0, :])
@@ -348,16 +330,15 @@ def tile_gcn_t_kernel(tc, x, mask, weight, bias, out):
         for c in range(CHUNKS):
             load_mask(3, c, c + 1)
             load_x(2, PAIR * c, PAIR * c + PAIR)
-        clear_diagonals(3)
         degree_spread(0)
         degree_resort(0)
         warm_clock(ones_b[:])
         warm_clock(ones_b[:])
-        degree_root(0)
-        degree_reciprocal(0)
+        degree_inverse_root(0)
         prepare(0)
         bias_matmul()
         nc.scalar.copy(out=bias_all[:], in_=bias_bank[:])
+        mask_diagonal(1, 0)
         column_sums(1, 0)
 
         def sums_due(r):
@@ -379,12 +360,12 @@ def tile_gcn_t_kernel(tc, x, mask, weight, bias, out):
                 for a in range(1, LEAD + 1):
                     prepare(a)
             for g, c in sums_due(r):
+                mask_diagonal(g, c)
                 column_sums(g, c)
             if r == 0:
                 continue
             if first_use:
                 add_bias(behind)
-                degree_reciprocal(next_graph)
             if ahead < ROUNDS:
                 scale_rows(ahead)
                 for s in range(PAIR):
@@ -406,7 +387,7 @@ def tile_gcn_t_kernel(tc, x, mask, weight, bias, out):
             if ahead == ROUNDS - 1:
                 relu_slice(behind, 0, "scalar")
             if finishing:
-                degree_root(next_graph)
+                degree_inverse_root(next_graph)
             if behind == ROUNDS - 1:
                 store(behind, 0, 1)
                 relu_slice(behind, 1, "vector")

@@ -110,8 +110,8 @@ def tile_gcn_t_kernel(tc, x, mask, weight, bias, out):
         bias_all = const.tile([P, OUTF], F32, name="bias_all")
         w_raw = const.tile([P, PASSES, PACK, OUTF], BF16, name="w_raw")
         w_grouped = const.tile([P, PASSES, OUTF, PACK], BF16, name="w_grouped", align_bytes=64)
-        w_words = const.tile([P, PASSES, OUTF], U32, name="w_words", align_bytes=64)
-        w_scales = const.tile([P, PASSES, OUTF], U8, name="w_scales", align_bytes=64)
+        w_words = const.tile([P, PASSES, OUTF], U32, name="w_words", align_bytes=256)
+        w_scales = const.tile([P, PASSES, OUTF], U8, name="w_scales", align_bytes=256)
         bias_bank = psum_o.tile([P, OUTF], F32, name="bias_bank", tag="o")
 
         def load_mask(g, first_chunk, end_chunk):
@@ -239,8 +239,8 @@ def tile_gcn_t_kernel(tc, x, mask, weight, bias, out):
 
         def quantise(r):
             width = PASSES * P
-            words = work.tile([P, PAIR * width], U32, name="words%d" % r, tag="words", align_bytes=64)
-            scales = work.tile([P, PAIR * width], U8, name="scales%d" % r, tag="scales", align_bytes=64)
+            words = work.tile([P, PAIR * width], U32, name="words%d" % r, tag="words", align_bytes=256)
+            scales = work.tile([P, PAIR * width], U8, name="scales%d" % r, tag="scales", align_bytes=256)
             packed[r] = (words, scales)
             if r in (0, ROUNDS - 1):
                 for s in range(PAIR):

@@ -30,7 +30,7 @@ LEAD = 2
 CHUNKS = 4
 CHUNK_ROWS = 2
 SUM_SLOT = 14
-SUM_COLS = 32
+SUM_COLS = 38
 SPREAD = P // SLICES
 RESIDENT = 3
 RESULT_BUFS = 12
@@ -113,6 +113,7 @@ def tile_gcn_t_kernel(tc, x, mask, weight, bias, out):
         w_words = const.tile([P, PASSES, OUTF], U32, name="w_words", align_bytes=256)
         w_scales = const.tile([P, PASSES, OUTF], U8, name="w_scales", align_bytes=256)
         bias_bank = psum_o.tile([P, OUTF], F32, name="bias_bank", tag="o")
+        warm_bank = psum_o.tile([P, OUTF], F32, name="warm_bank", tag="o")
 
         def load_mask(g, first_chunk, end_chunk):
             if g not in mask_tiles:
@@ -187,7 +188,7 @@ def tile_gcn_t_kernel(tc, x, mask, weight, bias, out):
             nc.tensor.matmul(out=bias_bank[:], lhsT=ones_b[:, 0:P], rhs=bias_row[:], start=True, stop=True)
 
         def warm_clock(columns):
-            nc.tensor.matmul(out=bias_bank[:], lhsT=ones_b[:, 0:P], rhs=columns, start=True, stop=True)
+            nc.tensor.matmul(out=warm_bank[:], lhsT=ones_b[:, 0:P], rhs=columns, start=True, stop=True)
 
         def weight_group(c, copy):
             copy(
@@ -294,6 +295,17 @@ def tile_gcn_t_kernel(tc, x, mask, weight, bias, out):
                 in_=results[r][:, first_slice:end_slice, :],
             )
 
+        def sum_chunk(g, c):
+            mask_diagonal(g, c)
+            column_sums(g, c)
+
+        def finish_degrees(g):
+            degree_spread(g)
+            if g == 0:
+                warm_clock(ones_b[:])
+            degree_resort(g)
+            degree_inverse_root(g)
+
         def prepare(r):
             scale_rows(r)
             for s in range(PAIR):
@@ -303,9 +315,9 @@ def tile_gcn_t_kernel(tc, x, mask, weight, bias, out):
 
         for c in range(PASSES):
             nc.sync.dma_start(out=w_raw[:, c], in_=weight_view[:, c])
+        nc.sync.dma_start(out=bias_row[0:1, :], in_=bias_view)
         load_mask(0, 0, CHUNKS)
         load_x(0, 0, PAIR)
-        nc.sync.dma_start(out=bias_row[0:1, :], in_=bias_view)
         load_mask(1, 0, 1)
         for c in range(1, CHUNKS):
             load_x(0, PAIR * c, PAIR * c + PAIR)
@@ -317,9 +329,11 @@ def tile_gcn_t_kernel(tc, x, mask, weight, bias, out):
         for c in range(PASSES):
             warm_clock(w_raw[:, c, 0, :])
             warm_clock(w_raw[:, c, 1, :])
+        bias_matmul()
         weight_group(0, nc.vector.tensor_copy)
         weight_group(1, nc.scalar.copy)
         weight_quantise(0)
+        nc.scalar.copy(out=bias_all[:], in_=bias_bank[:])
         for c in range(CHUNKS):
             mask_diagonal(0, c)
             if c == 1:
@@ -330,42 +344,30 @@ def tile_gcn_t_kernel(tc, x, mask, weight, bias, out):
         for c in range(CHUNKS):
             load_mask(3, c, c + 1)
             load_x(2, PAIR * c, PAIR * c + PAIR)
-        degree_spread(0)
-        degree_resort(0)
-        warm_clock(ones_b[:])
-        warm_clock(ones_b[:])
-        degree_inverse_root(0)
+        finish_degrees(0)
+        sum_chunk(1, 0)
         prepare(0)
-        bias_matmul()
-        nc.scalar.copy(out=bias_all[:], in_=bias_bank[:])
-        mask_diagonal(1, 0)
-        column_sums(1, 0)
-
-        def sums_due(r):
-            g, c = divmod(r + ROUNDS_PER_GRAPH + LEAD, ROUNDS_PER_GRAPH)
-            return ([(1, 1)] if r == 0 else []) + ([(g, c)] if g < GRAPHS else [])
+        prepare(1)
 
         for r in range(ROUNDS + 1):
             ahead = r + LEAD
             behind = r - 1
-            next_graph = r // ROUNDS_PER_GRAPH + 1
-            finishing = r % ROUNDS_PER_GRAPH == LEAD - 1 and next_graph < GRAPHS
-            first_use = r % ROUNDS_PER_GRAPH == LEAD and next_graph < GRAPHS
+            g, c = divmod(r + ROUNDS_PER_GRAPH + LEAD, ROUNDS_PER_GRAPH)
+            finishing = c == CHUNKS - 1 and 1 < g < GRAPHS
+            first_use = c == 0 and g <= GRAPHS
 
             if r < ROUNDS:
                 quantise(r)
                 for s in range(PAIR):
                     multiply_slice(r, s)
-            if r == 0:
-                for a in range(1, LEAD + 1):
-                    prepare(a)
-            for g, c in sums_due(r):
-                mask_diagonal(g, c)
-                column_sums(g, c)
-            if r == 0:
-                continue
             if first_use:
+                if r == LEAD:
+                    finish_degrees(1)
                 add_bias(behind)
+            if r < LEAD:
+                sum_chunk(1, r + 1)
+            elif g < GRAPHS:
+                sum_chunk(g, c)
             if ahead < ROUNDS:
                 scale_rows(ahead)
                 for s in range(PAIR):
@@ -373,25 +375,27 @@ def tile_gcn_t_kernel(tc, x, mask, weight, bias, out):
                 if ahead == ROUNDS_PER_GRAPH - 1:
                     load_x(3, 0, 4)
                     load_x(3, 4, 8)
-            if not first_use:
+            if behind >= 0 and not first_use:
                 add_bias(behind)
+            if r == LEAD - 1:
+                sum_chunk(1, CHUNKS - 1)
             if finishing:
-                degree_spread(next_graph)
-                degree_resort(next_graph)
+                degree_spread(g)
+                degree_resort(g)
             if ahead < ROUNDS:
                 group_slice(ahead, 0)
-            if ahead != ROUNDS - 1:
+            if behind >= 0 and ahead != ROUNDS - 1:
                 relu_slice(behind, 0, "scalar")
             if ahead < ROUNDS:
                 group_slice(ahead, 1)
             if ahead == ROUNDS - 1:
                 relu_slice(behind, 0, "scalar")
             if finishing:
-                degree_inverse_root(next_graph)
+                degree_inverse_root(g)
             if behind == ROUNDS - 1:
                 store(behind, 0, 1)
                 relu_slice(behind, 1, "vector")
                 store(behind, 1, 2)
-            else:
+            elif behind >= 0:
                 relu_slice(behind, 1, "scalar")
                 store(behind, 0, PAIR)

@@ -26,6 +26,7 @@ SLICES = NODES // P
 PAIR = 2
 ROUNDS_PER_GRAPH = SLICES // PAIR
 ROUNDS = GRAPHS * ROUNDS_PER_GRAPH
+SPLIT_STORES = 4
 LEAD = 2
 CHUNKS = 4
 CHUNK_ROWS = 2
@@ -392,9 +393,9 @@ def tile_gcn_t_kernel(tc, x, mask, weight, bias, out):
                 relu_slice(behind, 0, "scalar")
             if finishing:
                 degree_inverse_root(g)
-            if behind == ROUNDS - 1:
+            if behind >= ROUNDS - SPLIT_STORES:
                 store(behind, 0, 1)
-                relu_slice(behind, 1, "vector")
+                relu_slice(behind, 1, "scalar" if behind < ROUNDS - 1 else "vector")
                 store(behind, 1, 2)
             elif behind >= 0:
                 relu_slice(behind, 1, "scalar")

from contextlib import ExitStack

import concourse.mybir as mybir
from concourse.masks import make_identity

FP8X4 = mybir.dt.float8_e4m3fn_x4
BF16 = mybir.dt.bfloat16
F32 = mybir.dt.float32
U32 = mybir.dt.uint32
U8 = mybir.dt.uint8
ALU = mybir.AluOpType
ACT = mybir.ActivationFunctionType
AX = mybir.AxisListType

P = 128
PACK = 4
GRAPHS = 4
NODES = 1024
FEAT = 1024
OUTF = 512
PASSES = FEAT // (P * PACK)
BLOCKS = NODES // P
HALVES = 2
PAIR_COLS = FEAT // 2 // HALVES
SLICES = NODES // P
PAIR = 2
ROUNDS_PER_GRAPH = SLICES // PAIR
ROUNDS = GRAPHS * ROUNDS_PER_GRAPH
SPLIT_STORES = 4
LEAD = 2
CHUNKS = 4
CHUNK_ROWS = 2
SUM_SLOT = 14
SUM_COLS = 38
SPREAD = P // SLICES
RESIDENT = 3
RESULT_BUFS = 12
LOOP = 1.0
FLOPS = 2 * GRAPHS * NODES * FEAT * OUTF


def tile_gcn_t_kernel(tc, x, mask, weight, bias, out):
    nc = tc.nc
    x_view = x.rearrange("a b (p t) k -> (a b) p t k", t=SLICES)
    out_view = out.rearrange("a b (p t) o -> (a b) p t o", t=SLICES)
    mask_view = mask.rearrange("a b (c p t) i -> (a b) p c t i", c=CHUNKS, p=P, t=CHUNK_ROWS)
    weight_view = weight.rearrange("(c p t) o -> p c t o", c=PASSES, t=PACK, p=P)
    bias_view = bias.rearrange("(r n) -> r n", r=1)

    with ExitStack() as ctx:
        const = ctx.enter_context(tc.tile_pool(name="const", bufs=1))
        mask_pool = ctx.enter_context(tc.tile_pool(name="mask_pool", bufs=RESIDENT))
        x_pool = ctx.enter_context(tc.tile_pool(name="x_pool", bufs=RESIDENT))
        work = ctx.enter_context(tc.tile_pool(name="work", bufs=LEAD + 1))
        small = ctx.enter_context(tc.tile_pool(name="small", bufs=2))
        result_pool = ctx.enter_context(tc.tile_pool(name="result_pool", bufs=RESULT_BUFS))
        psum_t = ctx.enter_context(tc.psum_pool(name="psum_t", bufs=3))
        psum_o = ctx.enter_context(tc.psum_pool(name="psum_o", bufs=4))
        psum_d = ctx.enter_context(tc.psum_pool(name="psum_d", bufs=1))
        ctx.enter_context(tc.manual_schedule())

        mask_tiles = {}
        x_tiles = {}
        sum_banks = {}
        spread_tiles = {}
        sorted_degrees = {}
        inv_sqrt_d = {}
        scaled = {}
        flipped = {}
        grouped = {}
        packed = {}
        products = {}
        results = {}

        ident_f = const.tile([P, P], F32, name="ident_f")
        one_col = const.tile([P, 1], F32, name="one_col")
        nc.vector.memset(one_col[:], 1.0)
        ones_b = const.tile([P, OUTF], BF16, name="ones_b")
        nc.vector.memset(ones_b[:], 1.0)
        bias_row = const.tile([P, OUTF], BF16, name="bias_row")
        nc.vector.memset(bias_row[:], 0.0)
        first_root = const.tile([P, 1], F32, name="first_root")
        nc.scalar.activation(out=first_root[:], in_=one_col[:], func=ACT.Abs_reciprocal_sqrt)
        make_identity(nc, ident_f[:])
        off_diagonal = const.tile([P, CHUNK_ROWS, P * CHUNK_ROWS], BF16, name="off_diagonal")
        nc.gpsimd.memset(off_diagonal[:], 1.0)
        for t in range(CHUNK_ROWS):
            nc.gpsimd.affine_select(
                out=off_diagonal[:, t, :],
                in_=off_diagonal[:, t, :],
                pattern=[[-1, P * CHUNK_ROWS]],
                compare_op=ALU.not_equal,
                fill=0.0,
                base=t,
                channel_multiplier=CHUNK_ROWS,
            )
        row_in_group = const.tile([P, SLICES], F32, name="row_in_group")
        nc.vector.tensor_reduce(
            out=row_in_group[:],
            in_=ident_f[:].rearrange("p (q t) -> p t q", t=SLICES),
            axis=AX.X,
            op=ALU.add,
        )
        group_of_row = const.tile([P, SPREAD], F32, name="group_of_row")
        nc.vector.tensor_reduce(
            out=group_of_row[:],
            in_=ident_f[:].rearrange("p (q t) -> p q t", t=SLICES),
            axis=AX.X,
            op=ALU.add,
        )
        bias_all = const.tile([P, OUTF], F32, name="bias_all")
        w_raw = const.tile([P, PASSES, PACK, OUTF], BF16, name="w_raw")
        w_grouped = const.tile([P, PASSES, OUTF, PACK], BF16, name="w_grouped", align_bytes=64)
        w_words = const.tile([P, PASSES, OUTF], U32, name="w_words", align_bytes=256)
        w_scales = const.tile([P, PASSES, OUTF], U8, name="w_scales", align_bytes=256)
        bias_bank = psum_o.tile([P, OUTF], F32, name="bias_bank", tag="o")
        warm_bank = psum_o.tile([P, OUTF], F32, name="warm_bank", tag="o")

        def load_mask(g, first_chunk, end_chunk):
            if g not in mask_tiles:
                mask_tiles[g] = mask_pool.tile(
                    [P, CHUNKS, CHUNK_ROWS, NODES], BF16, name="mask%d" % g, tag="mask"
                )
            for c in range(first_chunk, end_chunk):
                nc.sync.dma_start(out=mask_tiles[g][:, c], in_=mask_view[g][:, c])

        def load_x(g, first_slice, end_slice):
            if g not in x_tiles:
                x_tiles[g] = x_pool.tile([P, SLICES, FEAT], BF16, name="x%d" % g, tag="x")
            rows = slice(first_slice, end_slice)
            nc.sync.dma_start(out=x_tiles[g][:, rows, :], in_=x_view[g][:, rows, :])

        def mask_diagonal(g, c):
            width = P * CHUNK_ROWS
            region = mask_tiles[g][:, c, :, c * width : (c + 1) * width]
            nc.vector.tensor_tensor(out=region, in0=region, in1=off_diagonal[:], op=ALU.mult)

        def column_sums(g, c):
            if c == 0:
                sum_banks[g] = psum_d.tile([P, OUTF], F32, name="sums%d" % g, tag="d")
            with_diagonal = [CHUNK_ROWS * c + t for t in range(CHUNK_ROWS)]
            for b in [b for b in range(BLOCKS) if b not in with_diagonal] + with_diagonal:
                first = (BLOCKS * c + b) * SUM_SLOT
                width = SUM_SLOT if b in with_diagonal else SUM_COLS
                for t in range(CHUNK_ROWS):
                    nc.tensor.matmul(
                        out=sum_banks[g][:, first : first + width],
                        lhsT=mask_tiles[g][:, c, t, b * P : (b + 1) * P],
                        rhs=ones_b[:, 0:width],
                        start=(t == 0),
                        stop=(t == CHUNK_ROWS - 1),
                    )

        def degree_spread(g):
            d_block = small.tile([P, BLOCKS], F32, name="d_block%d" % g, tag="d_block")
            nc.vector.tensor_reduce(
                out=d_block[:],
                in_=sum_banks[g][:, 0 : CHUNKS * BLOCKS * SUM_SLOT].rearrange(
                    "p (c b n) -> p b c n", c=CHUNKS, n=SUM_SLOT
                )[:, :, :, 0],
                axis=AX.X,
                op=ALU.add,
            )
            spread_tiles[g] = small.tile([P, BLOCKS, SPREAD], F32, name="spread%d" % g, tag="spread")
            nc.vector.scalar_tensor_tensor(
                out=spread_tiles[g][:],
                in0=d_block[:].unsqueeze(2).to_broadcast([P, BLOCKS, SPREAD]),
                scalar=LOOP,
                in1=group_of_row[:].unsqueeze(1).to_broadcast([P, BLOCKS, SPREAD]),
                op0=ALU.add,
                op1=ALU.mult,
            )

        def degree_resort(g):
            sorted_degrees[g] = psum_t.tile([P, SLICES], F32, name="sorted%d" % g, tag="t")
            nc.tensor.matmul(
                out=sorted_degrees[g][:],
                lhsT=spread_tiles[g][:].rearrange("p b q -> p (b q)"),
                rhs=row_in_group[:],
                start=True,
                stop=True,
            )

        def degree_inverse_root(g):
            inv_sqrt_d[g] = small.tile([P, SLICES], F32, name="inv_sqrt_d%d" % g, tag="inv_sqrt_d")
            nc.scalar.activation(out=inv_sqrt_d[g][:], in_=sorted_degrees[g][:], func=ACT.Abs_reciprocal_sqrt)

        def bias_matmul():
            nc.tensor.matmul(out=bias_bank[:], lhsT=ones_b[:, 0:P], rhs=bias_row[:], start=True, stop=True)

        def warm_clock(columns):
            nc.tensor.matmul(out=warm_bank[:], lhsT=ones_b[:, 0:P], rhs=columns, start=True, stop=True)

        def weight_group(c, copy):
            copy(
                out=w_grouped[:, c].rearrange("p (a i) t -> p a t i", i=4),
                in_=w_raw[:, c].rearrange("p t (a i) -> p a t i", i=4),
            )

        def weight_quantise(c):
            nc.vector.quantize_mx(
                out=w_words[:, c, :].bitcast(FP8X4),
                scales=w_scales[:, c, :],
                in_=w_grouped[:, c].rearrange("p o t -> p (o t)"),
            )

        def scale_rows(r):
            g, q = divmod(r, ROUNDS_PER_GRAPH)
            scaled[r] = work.tile([P, PAIR, HALVES, PAIR_COLS, 2], BF16, name="scaled%d" % r, tag="scaled")
            for s in range(PAIR):
                t = PAIR * q + s
                nc.vector.tensor_scalar(
                    out=scaled[r][:, s],
                    in0=x_tiles[g][:, t, :].rearrange("p (m u e) -> p u m e", u=HALVES, e=2),
                    scalar1=inv_sqrt_d[g][:, t : t + 1],
                    scalar2=None,
                    op0=ALU.mult,
                )

        def transpose_slice(r, s):
            bank = psum_t.tile([P, PASSES, HALVES, P], F32, name="flipped%d_%d" % (r, s), tag="t")
            flipped[(r, s)] = bank
            pairs = scaled[r][:, s].rearrange("p u m e -> p (u m e)").bitcast(F32)
            for c in range(PASSES):
                for u in range(HALVES):
                    first = u * PAIR_COLS + c * P
                    nc.tensor.transpose(bank[:, c, u, :], pairs[:, first : first + P], ident_f[:])

        def group_slice(r, s):
            if s == 0:
                grouped[r] = work.tile(
                    [P, PAIR, PASSES, P, PACK], BF16, name="grouped%d" % r, tag="grouped", align_bytes=64
                )
            nc.scalar.copy(
                out=grouped[r][:, s]
                .rearrange("p c i t -> p (c i t)")
                .bitcast(F32)
                .rearrange("p (c i u) -> p c i u", c=PASSES, u=HALVES),
                in_=flipped[(r, s)][:].rearrange("p c u i -> p c i u"),
            )

        def quantise(r):
            width = PASSES * P
            words = work.tile([P, PAIR * width], U32, name="words%d" % r, tag="words", align_bytes=256)
            scales = work.tile([P, PAIR * width], U8, name="scales%d" % r, tag="scales", align_bytes=256)
            packed[r] = (words, scales)
            if r in (0, ROUNDS - 1):
                for s in range(PAIR):
                    cols = slice(s * width, (s + 1) * width)
                    nc.vector.quantize_mx(
                        out=words[:, cols].bitcast(FP8X4),
                        scales=scales[:, cols],
                        in_=grouped[r][:, s].rearrange("p c i t -> p (c i t)"),
                    )
            else:
                nc.vector.quantize_mx(
                    out=words[:].bitcast(FP8X4),
                    scales=scales[:],
                    in_=grouped[r][:].rearrange("p s c i t -> p (s c i t)"),
                )

        def multiply_slice(r, s):
            words, scales = packed[r]
            bank = psum_o.tile([P, OUTF], F32, name="product%d_%d" % (r, s), tag="o")
            products[(r, s)] = bank
            for c in range(PASSES):
                cols = slice((PASSES * s + c) * P, (PASSES * s + c + 1) * P)
                nc.tensor.matmul_mx(
                    out=bank[:],
                    lhsT=words[:, cols].bitcast(FP8X4),
                    lhsT_scale=scales[:, cols],
                    rhs=w_words[:, c, :].bitcast(FP8X4),
                    rhs_scale=w_scales[:, c, :],
                    start=(c == 0),
                    stop=(c == PASSES - 1),
                )

        def add_bias(r):
            results[r] = result_pool.tile([P, PAIR, OUTF], F32, name="result%d" % r, tag="result")
            for s in range(PAIR):
                nc.vector.tensor_tensor(
                    out=results[r][:, s, :], in0=products[(r, s)][:], in1=bias_all[:], op=ALU.add
                )

        def relu_slice(r, s, engine):
            part = results[r][:, s, :]
            if engine == "scalar":
                nc.scalar.activation(out=part, in_=part, func=ACT.Relu)
            else:
                nc.vector.tensor_scalar_max(out=part, in0=part, scalar1=0.0)

        def store(r, first_slice, end_slice):
            g, q = divmod(r, ROUNDS_PER_GRAPH)
            nc.sync.dma_start(
                out=out_view[g][:, PAIR * q + first_slice : PAIR * q + end_slice, :],
                in_=results[r][:, first_slice:end_slice, :],
            )

        def sum_chunk(g, c):
            mask_diagonal(g, c)
            column_sums(g, c)

        def finish_degrees(g):
            degree_spread(g)
            if g == 0:
                warm_clock(ones_b[:])
            degree_resort(g)
            degree_inverse_root(g)

        def prepare(r):
            scale_rows(r)
            for s in range(PAIR):
                transpose_slice(r, s)
            for s in range(PAIR):
                group_slice(r, s)

        for c in range(PASSES):
            nc.sync.dma_start(out=w_raw[:, c], in_=weight_view[:, c])
        nc.sync.dma_start(out=bias_row[0:1, :], in_=bias_view)
        load_mask(0, 0, CHUNKS)
        load_x(0, 0, PAIR)
        load_mask(1, 0, 1)
        for c in range(1, CHUNKS):
            load_x(0, PAIR * c, PAIR * c + PAIR)
            load_mask(1, c, c + 1)
        for c in range(CHUNKS):
            load_mask(2, c, c + 1)
            load_x(1, PAIR * c, PAIR * c + PAIR)

        for c in range(PASSES):
            warm_clock(w_raw[:, c, 0, :])
            warm_clock(w_raw[:, c, 1, :])
        bias_matmul()
        weight_group(0, nc.vector.tensor_copy)
        weight_group(1, nc.scalar.copy)
        weight_quantise(0)
        nc.scalar.copy(out=bias_all[:], in_=bias_bank[:])
        for c in range(CHUNKS):
            mask_diagonal(0, c)
            if c == 1:
                weight_quantise(1)
            if c > 0:
                warm_clock(ones_b[:])
            column_sums(0, c)
        for c in range(CHUNKS):
            load_mask(3, c, c + 1)
            load_x(2, PAIR * c, PAIR * c + PAIR)
        finish_degrees(0)
        sum_chunk(1, 0)
        prepare(0)
        prepare(1)

        for r in range(ROUNDS + 1):
            ahead = r + LEAD
            behind = r - 1
            g, c = divmod(r + ROUNDS_PER_GRAPH + LEAD, ROUNDS_PER_GRAPH)
            finishing = c == CHUNKS - 1 and 1 < g < GRAPHS
            first_use = c == 0 and g <= GRAPHS

            if r < ROUNDS:
                quantise(r)
                for s in range(PAIR):
                    multiply_slice(r, s)
            if first_use:
                if r == LEAD:
                    finish_degrees(1)
                add_bias(behind)
            if r < LEAD:
                sum_chunk(1, r + 1)
            elif g < GRAPHS:
                sum_chunk(g, c)
            if ahead < ROUNDS:
                scale_rows(ahead)
                for s in range(PAIR):
                    transpose_slice(ahead, s)
                if ahead == ROUNDS_PER_GRAPH - 1:
                    load_x(3, 0, 4)
                    load_x(3, 4, 8)
            if behind >= 0 and not first_use:
                add_bias(behind)
            if r == LEAD - 1:
                sum_chunk(1, CHUNKS - 1)
            if finishing:
                degree_spread(g)
                degree_resort(g)
            if ahead < ROUNDS:
                group_slice(ahead, 0)
            if behind >= 0 and ahead != ROUNDS - 1:
                relu_slice(behind, 0, "scalar")
            if ahead < ROUNDS:
                group_slice(ahead, 1)
            if ahead == ROUNDS - 1:
                relu_slice(behind, 0, "scalar")
            if finishing:
                degree_inverse_root(g)
            if behind >= ROUNDS - SPLIT_STORES:
                store(behind, 0, 1)
                relu_slice(behind, 1, "scalar" if behind < ROUNDS - 1 else "vector")
                store(behind, 1, 2)
            elif behind >= 0:
                relu_slice(behind, 1, "scalar")
                store(behind, 0, PAIR)
